import numpy as np
import ml_dtypes


def mxq(x, axis, fmt="e4m3"):
    dtype, down = {"e4m3": (ml_dtypes.float8_e4m3fn, 7), "e5m2": (ml_dtypes.float8_e5m2, 14)}[fmt]
    v = np.moveaxis(np.asarray(x, np.float32).astype(ml_dtypes.bfloat16).astype(np.float64), axis, -1)
    blocks = v.reshape(v.shape[:-1] + (-1, 32))
    amax = np.abs(blocks).max(-1, keepdims=True)
    byte = np.maximum(np.where(amax > 0, np.frexp(amax)[1] - 1 + 127, 0) - down, 1)
    scale = np.exp2(byte - 127.0)
    codes = (blocks / scale).astype(np.float32).astype(dtype).astype(np.float64)
    return np.moveaxis((codes * scale).reshape(v.shape), -1, axis)


WIDE = False


def mx_kscale(k):
    if not WIDE:
        return np.ones(k)
    levels = np.array([10, -10, 5, -5, 0])
    a = np.random.permutation(np.resize(levels, k // 512 * 4)).reshape(k // 512, 4)
    idx = np.arange(k)
    return np.exp2(a[idx // 512, idx % 128 // 32])


BF16 = ml_dtypes.bfloat16


def bf(x):
    return np.asarray(x, np.float32).astype(BF16)


def f64(x):
    return np.asarray(x).astype(np.float64)


B, D_IN, D_FEAT, N_EX, N_LAB = 1024, 512, 512, 8192, 128
EPS = 1e-12


def l2_normalize(x):
    n = np.sqrt((x * x).sum(-1, keepdims=True))
    return x / np.maximum(n, EPS)


def setup_inputs():
    s = mx_kscale(D_IN)
    return {"features": bf(np.random.standard_normal((B, D_IN)) * s),
            "ex_features": bf(np.random.standard_normal((N_EX, D_IN)) * s),
            "g_weight": bf(np.random.standard_normal((D_FEAT, D_IN)) / np.sqrt(D_IN) / s)}


def reference(features, ex_features, g_weight):
    gq = mxq(f64(g_weight), 1, "e4m3")
    f = mxq(f64(features), 1, "e4m3") @ gq.T
    e = mxq(f64(ex_features), 1, "e4m3") @ gq.T
    return l2_normalize(f), l2_normalize(e)

@@ -1,0 +1,189 @@
+from contextlib import ExitStack
+
+import concourse.mybir as mybir
+from concourse.masks import make_identity
+
+F32 = mybir.dt.float32
+BF16 = mybir.dt.bfloat16
+U32 = mybir.dt.uint32
+U8 = mybir.dt.uint8
+FP8X4 = mybir.dt.float8_e4m3fn_x4
+ACT = mybir.ActivationFunctionType
+ALU = mybir.AluOpType
+
+P = 128
+K = 512
+N = 512
+WORDS = K // 2
+ROUND = 2
+GROUP = 8
+STORE_TILES = 4
+ACC_BANKS = 6
+FLIP_BANKS = 2
+VECTOR_REGROUPS_EVERY = 4
+EPS = 1e-12
+
+FLOPS = 2 * (1024 + 8192) * K * N
+
+
+def tile_minerva_pb_kernel(tc, features, ex_features, g_weight, out_0, out_1):
+    nc = tc.nc
+    with ExitStack() as ctx:
+        const = ctx.enter_context(tc.tile_pool(name="const", bufs=1))
+        rows_pool = ctx.enter_context(tc.tile_pool(name="rows", bufs=1))
+        grouped_pool = ctx.enter_context(tc.tile_pool(name="grouped", bufs=3))
+        operand_pool = ctx.enter_context(tc.tile_pool(name="operand", bufs=3))
+        norm_pool = ctx.enter_context(tc.tile_pool(name="norms", bufs=4))
+        result_pool = ctx.enter_context(tc.tile_pool(name="result", bufs=8))
+        flip_pool = ctx.enter_context(tc.psum_pool(name="flip", bufs=FLIP_BANKS))
+        acc_pool = ctx.enter_context(tc.psum_pool(name="acc", bufs=ACC_BANKS))
+        ctx.enter_context(tc.manual_schedule())
+
+        g_rows = const.tile([P, 4 * K], BF16, name="g_rows")
+        nc.sync.dma_start(
+            out=g_rows[:].rearrange("p (t k) -> p t k", k=K),
+            in_=g_weight.rearrange("(t p) k -> p t k", p=P),
+        )
+        x_words = []
+        out_views = []
+        for x, out in ((features, out_0), (ex_features, out_1)):
+            for base in range(0, x.shape[0], GROUP * P):
+                x_rows = rows_pool.tile([P, GROUP * K], BF16, name="x_rows%d" % len(out_views))
+                src = x[base : base + GROUP * P, :].rearrange("(p t) k -> p (t k)", t=GROUP)
+                pieces = 2 if len(out_views) == 0 else 1
+                width = GROUP * K // pieces
+                for c in range(pieces):
+                    cols = slice(c * width, (c + 1) * width)
+                    nc.sync.dma_start(out=x_rows[:, cols], in_=src[:, cols])
+                words = x_rows[:].bitcast(F32)
+                for h in range(GROUP // ROUND):
+                    x_words.append(words[:, h * ROUND * WORDS : (h + 1) * ROUND * WORDS])
+                dst = out[base : base + GROUP * P, :].rearrange("(p t) n -> p t n", t=GROUP)
+                for s in range(GROUP // STORE_TILES):
+                    out_views.append(dst[:, s * STORE_TILES : (s + 1) * STORE_TILES, :])
+        rounds = len(x_words)
+
+        identity = const.tile([P, P], F32, name="identity")
+        make_identity(nc, identity[:])
+
+        one = const.tile([P, 1], F32, name="one")
+        nc.vector.memset(one[:], 1.0)
+        root_of_one = const.tile([P, 1], F32, name="root_of_one")
+        nc.scalar.activation(out=root_of_one[:], in_=one[:], func=ACT.Sqrt)
+
+        def transposes(words):
+            flipped = flip_pool.tile([P, ROUND, 2, P], F32, name="flipped")
+            for j in range(ROUND):
+                for u in range(2):
+                    c = (2 * j + u) * P
+                    nc.tensor.transpose(flipped[:, j, u, :], words[:, c : c + P], identity[:])
+            return flipped
+
+        def regroup(flipped, on_vector):
+            grouped = grouped_pool.tile([P, ROUND * K], BF16, align_bytes=64, name="grouped")
+            dst = grouped[:].bitcast(F32).rearrange("p (j r u) -> p j r u", j=ROUND, u=2)
+            src = flipped[:].rearrange("p j u r -> p j r u")
+            if on_vector:
+                nc.vector.tensor_copy(out=dst, in_=src)
+            else:
+                nc.scalar.copy(out=dst, in_=src)
+            return grouped
+
+        def quantise(grouped, codes, scales):
+            nc.vector.quantize_mx(out=codes.bitcast(FP8X4), scales=scales, in_=grouped[:])
+
+        g_codes = const.tile([P, N], U32, align_bytes=64, name="g_codes")
+        g_scales = const.tile([P, N], U8, align_bytes=64, name="g_scales")
+        g_words = g_rows[:].bitcast(F32)
+        g_flipped = [
+            transposes(g_words[:, b * ROUND * WORDS : (b + 1) * ROUND * WORDS]) for b in range(2)
+        ]
+        g_grouped = [regroup(g_flipped[b], on_vector=(b == 1)) for b in range(2)]
+        for b in range(2):
+            cols = slice(b * ROUND * P, (b + 1) * ROUND * P)
+            quantise(g_grouped[b], g_codes[:, cols], g_scales[:, cols])
+
+        flipped_of = {}
+        grouped_of = {}
+        codes_of = {}
+        scales_of = {}
+        acc_of = {}
+        result_of = {}
+        sumsq_of = {}
+        norm_of = {}
+        clamped_of = {}
+        inverse_of = {}
+
+        def live(r):
+            return 0 <= r < rounds
+
+        lead = ACC_BANKS // ROUND - 1
+        for i in range(-lead - 2, rounds + 1):
+            if live(i - 1):
+                clamped = norm_pool.tile([P, ROUND], F32, name="clamped")
+                nc.vector.tensor_scalar(
+                    out=clamped[:], in0=norm_of[i - 1][:], scalar1=EPS, scalar2=None, op0=ALU.max
+                )
+                clamped_of[i - 1] = clamped
+            if live(i + lead):
+                codes = operand_pool.tile([P, ROUND * P], U32, align_bytes=64, name="codes")
+                scales = operand_pool.tile([P, ROUND * P], U8, align_bytes=64, name="scales")
+                quantise(grouped_of[i + lead], codes[:], scales[:])
+                codes_of[i + lead] = codes
+                scales_of[i + lead] = scales
+            if live(i - 1):
+                inverse = norm_pool.tile([P, ROUND], F32, name="inverse")
+                nc.vector.reciprocal(out=inverse[:], in_=clamped_of[i - 1][:])
+                inverse_of[i - 1] = inverse
+            if live(i):
+                sumsq = norm_pool.tile([P, ROUND], F32, name="sumsq")
+                sumsq_of[i] = sumsq
+            for j in range(ROUND):
+                if live(i - 1):
+                    t = (i - 1) * ROUND + j
+                    nc.vector.tensor_scalar(
+                        out=result_of[t // STORE_TILES][:, t % STORE_TILES, :],
+                        in0=acc_of[t][:],
+                        scalar1=inverse_of[i - 1][:, j : j + 1],
+                        scalar2=None,
+                        op0=ALU.mult,
+                    )
+                if live(i + lead):
+                    t = (i + lead) * ROUND + j
+                    acc = acc_pool.tile([P, N], F32, name="acc")
+                    rows = slice(j * P, (j + 1) * P)
+                    nc.tensor.matmul_mx(
+                        out=acc[:],
+                        lhsT=codes_of[i + lead][:, rows].bitcast(FP8X4),
+                        lhsT_scale=scales_of[i + lead][:, rows],
+                        rhs=g_codes[:].bitcast(FP8X4),
+                        rhs_scale=g_scales[:],
+                        start=True,
+                        stop=True,
+                    )
+                    acc_of[t] = acc
+                if live(i):
+                    t = i * ROUND + j
+                    if t % STORE_TILES == 0:
+                        result = result_pool.tile([P, STORE_TILES, N], F32, name="result")
+                        result_of[t // STORE_TILES] = result
+                    nc.scalar.activation(
+                        out=result_of[t // STORE_TILES][:, t % STORE_TILES, :],
+                        in_=acc_of[t][:],
+                        func=ACT.Square,
+                        accum_out=sumsq_of[i][:, j : j + 1],
+                    )
+            if live(i + lead + 1):
+                r = i + lead + 1
+                grouped_of[r] = regroup(
+                    flipped_of[r], on_vector=(r % VECTOR_REGROUPS_EVERY == VECTOR_REGROUPS_EVERY - 1)
+                )
+            if live(i):
+                norm = norm_pool.tile([P, ROUND], F32, name="norm")
+                nc.scalar.activation(out=norm[:], in_=sumsq_of[i][:], func=ACT.Sqrt)
+                norm_of[i] = norm
+            if live(i + lead + 2):
+                flipped_of[i + lead + 2] = transposes(x_words[i + lead + 2])
+            if live(i - 1) and (i * ROUND) % STORE_TILES == 0:
+                s = (i * ROUND) // STORE_TILES - 1
+                nc.sync.dma_start(out=out_views[s], in_=result_of[s][:])

@@ -15,11 +15,10 @@ P = 128
 K = 512
 N = 512
 WORDS = K // 2
-ROUND = 2
+PAIR = 2
 GROUP = 8
 STORE_TILES = 4
-ACC_BANKS = 6
-FLIP_BANKS = 2
+PSUM_BANKS = 8
 VECTOR_REGROUPS_EVERY = 4
 EPS = 1e-12
 
@@ -28,162 +27,134 @@ FLOPS = 2 * (1024 + 8192) * K * N
 
 def tile_minerva_pb_kernel(tc, features, ex_features, g_weight, out_0, out_1):
     nc = tc.nc
+    row_tiles = (features.shape[0] + ex_features.shape[0]) // P
     with ExitStack() as ctx:
         const = ctx.enter_context(tc.tile_pool(name="const", bufs=1))
         rows_pool = ctx.enter_context(tc.tile_pool(name="rows", bufs=1))
-        grouped_pool = ctx.enter_context(tc.tile_pool(name="grouped", bufs=3))
-        operand_pool = ctx.enter_context(tc.tile_pool(name="operand", bufs=3))
-        norm_pool = ctx.enter_context(tc.tile_pool(name="norms", bufs=4))
+        grouped_pool = ctx.enter_context(tc.tile_pool(name="grouped", bufs=6))
+        norm_pool = ctx.enter_context(tc.tile_pool(name="norms", bufs=6))
         result_pool = ctx.enter_context(tc.tile_pool(name="result", bufs=8))
-        flip_pool = ctx.enter_context(tc.psum_pool(name="flip", bufs=FLIP_BANKS))
-        acc_pool = ctx.enter_context(tc.psum_pool(name="acc", bufs=ACC_BANKS))
+        psum = ctx.enter_context(tc.psum_pool(name="psum", bufs=PSUM_BANKS))
         ctx.enter_context(tc.manual_schedule())
 
         g_rows = const.tile([P, 4 * K], BF16, name="g_rows")
-        nc.sync.dma_start(
-            out=g_rows[:].rearrange("p (t k) -> p t k", k=K),
-            in_=g_weight.rearrange("(t p) k -> p t k", p=P),
-        )
+        g_src = g_weight.rearrange("(t p) k -> p t k", p=P)
+        g_dst = g_rows[:].rearrange("p (t k) -> p t k", k=K)
+        for b in range(2):
+            nc.sync.dma_start(
+                out=g_dst[:, b * PAIR : (b + 1) * PAIR, :], in_=g_src[:, b * PAIR : (b + 1) * PAIR, :]
+            )
         x_words = []
         out_views = []
         for x, out in ((features, out_0), (ex_features, out_1)):
             for base in range(0, x.shape[0], GROUP * P):
                 x_rows = rows_pool.tile([P, GROUP * K], BF16, name="x_rows%d" % len(out_views))
                 src = x[base : base + GROUP * P, :].rearrange("(p t) k -> p (t k)", t=GROUP)
-                pieces = 2 if len(out_views) == 0 else 1
+                pieces = 4 if len(out_views) == 0 else 1
                 width = GROUP * K // pieces
                 for c in range(pieces):
                     cols = slice(c * width, (c + 1) * width)
                     nc.sync.dma_start(out=x_rows[:, cols], in_=src[:, cols])
                 words = x_rows[:].bitcast(F32)
-                for h in range(GROUP // ROUND):
-                    x_words.append(words[:, h * ROUND * WORDS : (h + 1) * ROUND * WORDS])
-                dst = out[base : base + GROUP * P, :].rearrange("(p t) n -> p t n", t=GROUP)
-                for s in range(GROUP // STORE_TILES):
-                    out_views.append(dst[:, s * STORE_TILES : (s + 1) * STORE_TILES, :])
-        rounds = len(x_words)
+                for h in range(GROUP // PAIR):
+                    x_words.append(words[:, h * PAIR * WORDS : (h + 1) * PAIR * WORDS])
+                out_views.append(
+                    out[base : base + GROUP * P, :].rearrange("(p t) n -> p t n", t=GROUP)
+                )
 
         identity = const.tile([P, P], F32, name="identity")
         make_identity(nc, identity[:])
 
-        one = const.tile([P, 1], F32, name="one")
-        nc.vector.memset(one[:], 1.0)
-        root_of_one = const.tile([P, 1], F32, name="root_of_one")
-        nc.scalar.activation(out=root_of_one[:], in_=one[:], func=ACT.Sqrt)
+        minus_half = const.tile([P, PAIR], F32, name="minus_half")
+        nc.vector.memset(minus_half[:], -0.5)
 
-        def transposes(words):
-            flipped = flip_pool.tile([P, ROUND, 2, P], F32, name="flipped")
-            for j in range(ROUND):
-                for u in range(2):
-                    c = (2 * j + u) * P
-                    nc.tensor.transpose(flipped[:, j, u, :], words[:, c : c + P], identity[:])
-            return flipped
+        g_codes = const.tile([P, N], U32, align_bytes=64, name="g_codes")
+        g_scales = const.tile([P, N], U8, align_bytes=64, name="g_scales")
+        x_codes = const.tile([P, row_tiles * P], U32, align_bytes=64, name="x_codes")
+        x_scales = const.tile([P, row_tiles * P], U8, align_bytes=64, name="x_scales")
 
-        def regroup(flipped, on_vector):
-            grouped = grouped_pool.tile([P, ROUND * K], BF16, align_bytes=64, name="grouped")
-            dst = grouped[:].bitcast(F32).rearrange("p (j r u) -> p j r u", j=ROUND, u=2)
-            src = flipped[:].rearrange("p j u r -> p j r u")
-            if on_vector:
-                nc.vector.tensor_copy(out=dst, in_=src)
-            else:
-                nc.scalar.copy(out=dst, in_=src)
-            return grouped
+        g_words = g_rows[:].bitcast(F32)
+        units = []
+        for b in range(2):
+            cols = slice(b * PAIR * P, (b + 1) * PAIR * P)
+            units.append(
+                (g_words[:, b * PAIR * WORDS : (b + 1) * PAIR * WORDS], g_codes[:, cols], g_scales[:, cols])
+            )
+        for r in range(row_tiles // PAIR):
+            cols = slice(r * PAIR * P, (r + 1) * PAIR * P)
+            units.append((x_words[r], x_codes[:, cols], x_scales[:, cols]))
 
         def quantise(grouped, codes, scales):
             nc.vector.quantize_mx(out=codes.bitcast(FP8X4), scales=scales, in_=grouped[:])
 
-        g_codes = const.tile([P, N], U32, align_bytes=64, name="g_codes")
-        g_scales = const.tile([P, N], U8, align_bytes=64, name="g_scales")
-        g_words = g_rows[:].bitcast(F32)
-        g_flipped = [
-            transposes(g_words[:, b * ROUND * WORDS : (b + 1) * ROUND * WORDS]) for b in range(2)
-        ]
-        g_grouped = [regroup(g_flipped[b], on_vector=(b == 1)) for b in range(2)]
-        for b in range(2):
-            cols = slice(b * ROUND * P, (b + 1) * ROUND * P)
-            quantise(g_grouped[b], g_codes[:, cols], g_scales[:, cols])
+        waiting = None
+        for i, (words, codes, scales) in enumerate(units):
+            flipped = psum.tile([P, PAIR, 2, P], F32, name="flipped", tag="bank")
+            for j in range(PAIR):
+                for u in range(2):
+                    c = (2 * j + u) * P
+                    nc.tensor.transpose(flipped[:, j, u, :], words[:, c : c + P], identity[:])
+            grouped = grouped_pool.tile([P, PAIR * K], BF16, align_bytes=64, name="grouped")
+            dst = grouped[:].bitcast(F32).rearrange("p (j r u) -> p j r u", j=PAIR, u=2)
+            src = flipped[:].rearrange("p j u r -> p j r u")
+            if i % VECTOR_REGROUPS_EVERY == VECTOR_REGROUPS_EVERY - 1:
+                nc.vector.tensor_copy(out=dst, in_=src)
+            else:
+                nc.scalar.copy(out=dst, in_=src)
+            if waiting is not None:
+                quantise(*waiting)
+            waiting = (grouped, codes, scales)
+        quantise(*waiting)
 
-        flipped_of = {}
-        grouped_of = {}
-        codes_of = {}
-        scales_of = {}
-        acc_of = {}
-        result_of = {}
-        sumsq_of = {}
-        norm_of = {}
-        clamped_of = {}
-        inverse_of = {}
+        result = None
+        for first in range(0, row_tiles, PAIR):
+            if first % STORE_TILES == 0:
+                result = result_pool.tile([P, STORE_TILES, N], F32, name="result")
+            sumsq = norm_pool.tile([P, PAIR], F32, name="sumsq")
+            products = []
+            for j in range(PAIR):
+                rows = slice((first + j) * P, (first + j + 1) * P)
+                acc = psum.tile([P, N], F32, name="acc", tag="bank")
+                nc.tensor.matmul_mx(
+                    out=acc[:],
+                    lhsT=x_codes[:, rows].bitcast(FP8X4),
+                    lhsT_scale=x_scales[:, rows],
+                    rhs=g_codes[:].bitcast(FP8X4),
+                    rhs_scale=g_scales[:],
+                    start=True,
+                    stop=True,
+                )
+                nc.scalar.activation(
+                    out=result[:, (first + j) % STORE_TILES, :],
+                    in_=acc[:],
+                    func=ACT.Square,
+                    accum_out=sumsq[:, j : j + 1],
+                )
+                products.append(acc)
 
-        def live(r):
-            return 0 <= r < rounds
+            floored = norm_pool.tile([P, PAIR], F32, name="floored")
+            nc.gpsimd.tensor_scalar(
+                out=floored[:], in0=sumsq[:], scalar1=EPS * EPS, scalar2=None, op0=ALU.max
+            )
+            inverse = norm_pool.tile([P, PAIR], F32, name="inverse")
+            nc.gpsimd.tensor_tensor(out=inverse[:], in0=floored[:], in1=minus_half[:], op=ALU.pow)
 
-        lead = ACC_BANKS // ROUND - 1
-        for i in range(-lead - 2, rounds + 1):
-            if live(i - 1):
-                clamped = norm_pool.tile([P, ROUND], F32, name="clamped")
+            for j in range(PAIR):
                 nc.vector.tensor_scalar(
-                    out=clamped[:], in0=norm_of[i - 1][:], scalar1=EPS, scalar2=None, op0=ALU.max
+                    out=result[:, (first + j) % STORE_TILES, :],
+                    in0=products[j][:],
+                    scalar1=inverse[:, j : j + 1],
+                    scalar2=None,
+                    op0=ALU.mult,
                 )
-                clamped_of[i - 1] = clamped
-            if live(i + lead):
-                codes = operand_pool.tile([P, ROUND * P], U32, align_bytes=64, name="codes")
-                scales = operand_pool.tile([P, ROUND * P], U8, align_bytes=64, name="scales")
-                quantise(grouped_of[i + lead], codes[:], scales[:])
-                codes_of[i + lead] = codes
-                scales_of[i + lead] = scales
-            if live(i - 1):
-                inverse = norm_pool.tile([P, ROUND], F32, name="inverse")
-                nc.vector.reciprocal(out=inverse[:], in_=clamped_of[i - 1][:])
-                inverse_of[i - 1] = inverse
-            if live(i):
-                sumsq = norm_pool.tile([P, ROUND], F32, name="sumsq")
-                sumsq_of[i] = sumsq
-            for j in range(ROUND):
-                if live(i - 1):
-                    t = (i - 1) * ROUND + j
-                    nc.vector.tensor_scalar(
-                        out=result_of[t // STORE_TILES][:, t % STORE_TILES, :],
-                        in0=acc_of[t][:],
-                        scalar1=inverse_of[i - 1][:, j : j + 1],
-                        scalar2=None,
-                        op0=ALU.mult,
-                    )
-                if live(i + lead):
-                    t = (i + lead) * ROUND + j
-                    acc = acc_pool.tile([P, N], F32, name="acc")
-                    rows = slice(j * P, (j + 1) * P)
-                    nc.tensor.matmul_mx(
-                        out=acc[:],
-                        lhsT=codes_of[i + lead][:, rows].bitcast(FP8X4),
-                        lhsT_scale=scales_of[i + lead][:, rows],
-                        rhs=g_codes[:].bitcast(FP8X4),
-                        rhs_scale=g_scales[:],
-                        start=True,
-                        stop=True,
-                    )
-                    acc_of[t] = acc
-                if live(i):
-                    t = i * ROUND + j
-                    if t % STORE_TILES == 0:
-                        result = result_pool.tile([P, STORE_TILES, N], F32, name="result")
-                        result_of[t // STORE_TILES] = result
-                    nc.scalar.activation(
-                        out=result_of[t // STORE_TILES][:, t % STORE_TILES, :],
-                        in_=acc_of[t][:],
-                        func=ACT.Square,
-                        accum_out=sumsq_of[i][:, j : j + 1],
-                    )
-            if live(i + lead + 1):
-                r = i + lead + 1
-                grouped_of[r] = regroup(
-                    flipped_of[r], on_vector=(r % VECTOR_REGROUPS_EVERY == VECTOR_REGROUPS_EVERY - 1)
+
+            done = first + PAIR
+            in_last_store = done > row_tiles - STORE_TILES
+            if in_last_store or done % STORE_TILES == 0:
+                count = PAIR if in_last_store else STORE_TILES
+                t0 = (done - count) % GROUP
+                s0 = (done - count) % STORE_TILES
+                nc.sync.dma_start(
+                    out=out_views[(done - 1) // GROUP][:, t0 : t0 + count, :],
+                    in_=result[:, s0 : s0 + count, :],
                 )
-            if live(i):
-                norm = norm_pool.tile([P, ROUND], F32, name="norm")
-                nc.scalar.activation(out=norm[:], in_=sumsq_of[i][:], func=ACT.Sqrt)
-                norm_of[i] = norm
-            if live(i + lead + 2):
-                flipped_of[i + lead + 2] = transposes(x_words[i + lead + 2])
-            if live(i - 1) and (i * ROUND) % STORE_TILES == 0:
-                s = (i * ROUND) // STORE_TILES - 1
-                nc.sync.dma_start(out=out_views[s], in_=result_of[s][:])

@@ -19,6 +19,10 @@ PAIR = 2
 GROUP = 8
 STORE_TILES = 4
 PSUM_BANKS = 8
+FLIP_BANKS = 2
+PRODUCT_BANKS = PSUM_BANKS - FLIP_BANKS
+FRONT_PER_STEP = 1
+FRONT_LEAD = 6
 VECTOR_REGROUPS_EVERY = 4
 EPS = 1e-12
 
@@ -28,13 +32,14 @@ FLOPS = 2 * (1024 + 8192) * K * N
 def tile_minerva_pb_kernel(tc, features, ex_features, g_weight, out_0, out_1):
     nc = tc.nc
     row_tiles = (features.shape[0] + ex_features.shape[0]) // P
+    pairs = row_tiles // PAIR
     with ExitStack() as ctx:
         const = ctx.enter_context(tc.tile_pool(name="const", bufs=1))
         rows_pool = ctx.enter_context(tc.tile_pool(name="rows", bufs=1))
-        grouped_pool = ctx.enter_context(tc.tile_pool(name="grouped", bufs=6))
-        norm_pool = ctx.enter_context(tc.tile_pool(name="norms", bufs=6))
+        grouped_pool = ctx.enter_context(tc.tile_pool(name="grouped", bufs=4))
+        norm_pool = ctx.enter_context(tc.tile_pool(name="norms", bufs=4))
         result_pool = ctx.enter_context(tc.tile_pool(name="result", bufs=8))
-        psum = ctx.enter_context(tc.psum_pool(name="psum", bufs=PSUM_BANKS))
+        psum = ctx.enter_context(tc.psum_pool(name="psum", bufs=1))
         ctx.enter_context(tc.manual_schedule())
 
         g_rows = const.tile([P, 4 * K], BF16, name="g_rows")
@@ -80,41 +85,55 @@ def tile_minerva_pb_kernel(tc, features, ex_features, g_weight, out_0, out_1):
             units.append(
                 (g_words[:, b * PAIR * WORDS : (b + 1) * PAIR * WORDS], g_codes[:, cols], g_scales[:, cols])
             )
-        for r in range(row_tiles // PAIR):
+        for r in range(pairs):
             cols = slice(r * PAIR * P, (r + 1) * PAIR * P)
             units.append((x_words[r], x_codes[:, cols], x_scales[:, cols]))
 
-        def quantise(grouped, codes, scales):
-            nc.vector.quantize_mx(out=codes.bitcast(FP8X4), scales=scales, in_=grouped[:])
+        flipped_of = {}
+        grouped_of = {}
 
-        waiting = None
-        for i, (words, codes, scales) in enumerate(units):
-            flipped = psum.tile([P, PAIR, 2, P], F32, name="flipped", tag="bank")
+        def flip(u):
+            bank = u if u < PRODUCT_BANKS else PRODUCT_BANKS + u % FLIP_BANKS
+            flipped = psum.tile([P, PAIR, 2, P], F32, name="flipped", tag="bank%d" % bank)
+            words = units[u][0]
             for j in range(PAIR):
-                for u in range(2):
-                    c = (2 * j + u) * P
-                    nc.tensor.transpose(flipped[:, j, u, :], words[:, c : c + P], identity[:])
+                for h in range(2):
+                    c = (2 * j + h) * P
+                    nc.tensor.transpose(flipped[:, j, h, :], words[:, c : c + P], identity[:])
+            flipped_of[u] = flipped
+
+        def regroup(u):
             grouped = grouped_pool.tile([P, PAIR * K], BF16, align_bytes=64, name="grouped")
-            dst = grouped[:].bitcast(F32).rearrange("p (j r u) -> p j r u", j=PAIR, u=2)
-            src = flipped[:].rearrange("p j u r -> p j r u")
-            if i % VECTOR_REGROUPS_EVERY == VECTOR_REGROUPS_EVERY - 1:
+            dst = grouped[:].bitcast(F32).rearrange("p (j r h) -> p j r h", j=PAIR, h=2)
+            src = flipped_of[u][:].rearrange("p j h r -> p j r h")
+            if u % VECTOR_REGROUPS_EVERY == 1:
                 nc.vector.tensor_copy(out=dst, in_=src)
             else:
                 nc.scalar.copy(out=dst, in_=src)
-            if waiting is not None:
-                quantise(*waiting)
-            waiting = (grouped, codes, scales)
-        quantise(*waiting)
+            grouped_of[u] = grouped
 
-        result = None
-        for first in range(0, row_tiles, PAIR):
-            if first % STORE_TILES == 0:
-                result = result_pool.tile([P, STORE_TILES, N], F32, name="result")
-            sumsq = norm_pool.tile([P, PAIR], F32, name="sumsq")
-            products = []
+        def quantise(u):
+            nc.vector.quantize_mx(
+                out=units[u][1].bitcast(FP8X4), scales=units[u][2], in_=grouped_of[u][:]
+            )
+
+        def front(u):
+            if u < len(units):
+                flip(u)
+            if 0 <= u - 1 < len(units):
+                regroup(u - 1)
+            if 0 <= u - 2 < len(units):
+                quantise(u - 2)
+
+        products_of = {}
+        result_of = {}
+        inverse_of = {}
+
+        def multiply(r, banks):
+            products_of[r] = []
             for j in range(PAIR):
-                rows = slice((first + j) * P, (first + j + 1) * P)
-                acc = psum.tile([P, N], F32, name="acc", tag="bank")
+                rows = slice((r * PAIR + j) * P, (r * PAIR + j + 1) * P)
+                acc = psum.tile([P, N], F32, name="acc", tag="bank%d" % banks[j])
                 nc.tensor.matmul_mx(
                     out=acc[:],
                     lhsT=x_codes[:, rows].bitcast(FP8X4),
@@ -124,31 +143,40 @@ def tile_minerva_pb_kernel(tc, features, ex_features, g_weight, out_0, out_1):
                     start=True,
                     stop=True,
                 )
+                products_of[r].append(acc)
+
+        def inverse_norms(r):
+            s = r * PAIR // STORE_TILES
+            if r * PAIR % STORE_TILES == 0:
+                result = result_pool.tile([P, STORE_TILES, N], F32, name="result")
+                result_of[s] = result
+            sumsq = norm_pool.tile([P, PAIR], F32, name="sumsq")
+            for j in range(PAIR):
                 nc.scalar.activation(
-                    out=result[:, (first + j) % STORE_TILES, :],
-                    in_=acc[:],
+                    out=result_of[s][:, (r * PAIR + j) % STORE_TILES, :],
+                    in_=products_of[r][j][:],
                     func=ACT.Square,
                     accum_out=sumsq[:, j : j + 1],
                 )
-                products.append(acc)
-
             floored = norm_pool.tile([P, PAIR], F32, name="floored")
             nc.gpsimd.tensor_scalar(
                 out=floored[:], in0=sumsq[:], scalar1=EPS * EPS, scalar2=None, op0=ALU.max
             )
             inverse = norm_pool.tile([P, PAIR], F32, name="inverse")
             nc.gpsimd.tensor_tensor(out=inverse[:], in0=floored[:], in1=minus_half[:], op=ALU.pow)
+            inverse_of[r] = inverse
 
+        def scale_and_store(r):
+            s = r * PAIR // STORE_TILES
             for j in range(PAIR):
                 nc.vector.tensor_scalar(
-                    out=result[:, (first + j) % STORE_TILES, :],
-                    in0=products[j][:],
-                    scalar1=inverse[:, j : j + 1],
+                    out=result_of[s][:, (r * PAIR + j) % STORE_TILES, :],
+                    in0=products_of[r][j][:],
+                    scalar1=inverse_of[r][:, j : j + 1],
                     scalar2=None,
                     op0=ALU.mult,
                 )
-
-            done = first + PAIR
+            done = (r + 1) * PAIR
             in_last_store = done > row_tiles - STORE_TILES
             if in_last_store or done % STORE_TILES == 0:
                 count = PAIR if in_last_store else STORE_TILES
@@ -156,5 +184,22 @@ def tile_minerva_pb_kernel(tc, features, ex_features, g_weight, out_0, out_1):
                 s0 = (done - count) % STORE_TILES
                 nc.sync.dma_start(
                     out=out_views[(done - 1) // GROUP][:, t0 : t0 + count, :],
-                    in_=result[:, s0 : s0 + count, :],
+                    in_=result_of[s][:, s0 : s0 + count, :],
                 )
+
+        for u in range(FRONT_LEAD):
+            front(u)
+        ring = list(range(PRODUCT_BANKS))
+        for i in range(pairs + 2):
+            entered = FRONT_LEAD + FRONT_PER_STEP * i
+            if entered - 1 >= len(units) and len(ring) == PRODUCT_BANKS:
+                ring = list(range(PRODUCT_BANKS, PSUM_BANKS)) + ring
+            if 0 <= i - 2:
+                scale_and_store(i - 2)
+            if i < pairs:
+                multiply(i, ring[:PAIR])
+                ring = ring[PAIR:] + ring[:PAIR]
+            if 0 <= i - 1 < pairs:
+                inverse_norms(i - 1)
+            for u in range(entered, entered + FRONT_PER_STEP):
+                front(u)

@@ -15,15 +15,15 @@ P = 128
 K = 512
 N = 512
 WORDS = K // 2
-PAIR = 2
+UNIT = 2
+G_UNITS = N // (UNIT * P)
 GROUP = 8
 STORE_TILES = 4
 PSUM_BANKS = 8
 FLIP_BANKS = 2
 PRODUCT_BANKS = PSUM_BANKS - FLIP_BANKS
-FRONT_PER_STEP = 1
-FRONT_LEAD = 6
-VECTOR_REGROUPS_EVERY = 4
+FRONT_LEAD = G_UNITS + 4
+VECTOR_COPIES_EVERY = 4
 EPS = 1e-12
 
 FLOPS = 2 * (1024 + 8192) * K * N
@@ -32,37 +32,36 @@ FLOPS = 2 * (1024 + 8192) * K * N
 def tile_minerva_pb_kernel(tc, features, ex_features, g_weight, out_0, out_1):
     nc = tc.nc
     row_tiles = (features.shape[0] + ex_features.shape[0]) // P
-    pairs = row_tiles // PAIR
+    pairs = row_tiles // UNIT
     with ExitStack() as ctx:
         const = ctx.enter_context(tc.tile_pool(name="const", bufs=1))
         rows_pool = ctx.enter_context(tc.tile_pool(name="rows", bufs=1))
-        grouped_pool = ctx.enter_context(tc.tile_pool(name="grouped", bufs=4))
-        norm_pool = ctx.enter_context(tc.tile_pool(name="norms", bufs=4))
+        grouped_pool = ctx.enter_context(tc.tile_pool(name="grouped", bufs=3))
+        norm_pool = ctx.enter_context(tc.tile_pool(name="norms", bufs=3))
         result_pool = ctx.enter_context(tc.tile_pool(name="result", bufs=8))
         psum = ctx.enter_context(tc.psum_pool(name="psum", bufs=1))
         ctx.enter_context(tc.manual_schedule())
 
-        g_rows = const.tile([P, 4 * K], BF16, name="g_rows")
+        g_rows = const.tile([P, G_UNITS * UNIT * K], BF16, name="g_rows")
         g_src = g_weight.rearrange("(t p) k -> p t k", p=P)
         g_dst = g_rows[:].rearrange("p (t k) -> p t k", k=K)
-        for b in range(2):
-            nc.sync.dma_start(
-                out=g_dst[:, b * PAIR : (b + 1) * PAIR, :], in_=g_src[:, b * PAIR : (b + 1) * PAIR, :]
-            )
+        for b in range(G_UNITS):
+            tiles = slice(b * UNIT, (b + 1) * UNIT)
+            nc.sync.dma_start(out=g_dst[:, tiles, :], in_=g_src[:, tiles, :])
         x_words = []
         out_views = []
         for x, out in ((features, out_0), (ex_features, out_1)):
             for base in range(0, x.shape[0], GROUP * P):
                 x_rows = rows_pool.tile([P, GROUP * K], BF16, name="x_rows%d" % len(out_views))
                 src = x[base : base + GROUP * P, :].rearrange("(p t) k -> p (t k)", t=GROUP)
-                pieces = 4 if len(out_views) == 0 else 1
+                pieces = GROUP // UNIT if len(out_views) == 0 else 1
                 width = GROUP * K // pieces
                 for c in range(pieces):
                     cols = slice(c * width, (c + 1) * width)
                     nc.sync.dma_start(out=x_rows[:, cols], in_=src[:, cols])
                 words = x_rows[:].bitcast(F32)
-                for h in range(GROUP // PAIR):
-                    x_words.append(words[:, h * PAIR * WORDS : (h + 1) * PAIR * WORDS])
+                for c in range(GROUP // UNIT):
+                    x_words.append(words[:, c * UNIT * WORDS : (c + 1) * UNIT * WORDS])
                 out_views.append(
                     out[base : base + GROUP * P, :].rearrange("(p t) n -> p t n", t=GROUP)
                 )
@@ -70,7 +69,7 @@ def tile_minerva_pb_kernel(tc, features, ex_features, g_weight, out_0, out_1):
         identity = const.tile([P, P], F32, name="identity")
         make_identity(nc, identity[:])
 
-        minus_half = const.tile([P, PAIR], F32, name="minus_half")
+        minus_half = const.tile([P, UNIT], F32, name="minus_half")
         nc.vector.memset(minus_half[:], -0.5)
 
         g_codes = const.tile([P, N], U32, align_bytes=64, name="g_codes")
@@ -80,33 +79,32 @@ def tile_minerva_pb_kernel(tc, features, ex_features, g_weight, out_0, out_1):
 
         g_words = g_rows[:].bitcast(F32)
         units = []
-        for b in range(2):
-            cols = slice(b * PAIR * P, (b + 1) * PAIR * P)
-            units.append(
-                (g_words[:, b * PAIR * WORDS : (b + 1) * PAIR * WORDS], g_codes[:, cols], g_scales[:, cols])
-            )
-        for r in range(pairs):
-            cols = slice(r * PAIR * P, (r + 1) * PAIR * P)
-            units.append((x_words[r], x_codes[:, cols], x_scales[:, cols]))
+        for b in range(G_UNITS):
+            cols = slice(b * UNIT * P, (b + 1) * UNIT * P)
+            words = g_words[:, b * UNIT * WORDS : (b + 1) * UNIT * WORDS]
+            units.append((words, g_codes[:, cols], g_scales[:, cols]))
+        for pair in range(pairs):
+            cols = slice(pair * UNIT * P, (pair + 1) * UNIT * P)
+            units.append((x_words[pair], x_codes[:, cols], x_scales[:, cols]))
 
         flipped_of = {}
         grouped_of = {}
 
-        def flip(u):
+        def transpose(u):
             bank = u if u < PRODUCT_BANKS else PRODUCT_BANKS + u % FLIP_BANKS
-            flipped = psum.tile([P, PAIR, 2, P], F32, name="flipped", tag="bank%d" % bank)
+            flipped = psum.tile([P, UNIT, 2, P], F32, name="flipped", tag="bank%d" % bank)
             words = units[u][0]
-            for j in range(PAIR):
+            for j in range(UNIT):
                 for h in range(2):
                     c = (2 * j + h) * P
                     nc.tensor.transpose(flipped[:, j, h, :], words[:, c : c + P], identity[:])
             flipped_of[u] = flipped
 
-        def regroup(u):
-            grouped = grouped_pool.tile([P, PAIR * K], BF16, align_bytes=64, name="grouped")
-            dst = grouped[:].bitcast(F32).rearrange("p (j r h) -> p j r h", j=PAIR, h=2)
-            src = flipped_of[u][:].rearrange("p j h r -> p j r h")
-            if u % VECTOR_REGROUPS_EVERY == 1:
+        def copy_out(u):
+            grouped = grouped_pool.tile([P, UNIT * K], BF16, align_bytes=64, name="grouped")
+            dst = grouped[:].bitcast(F32).rearrange("p (j row h) -> p j row h", j=UNIT, h=2)
+            src = flipped_of[u][:].rearrange("p j h row -> p j row h")
+            if u % VECTOR_COPIES_EVERY == 0:
                 nc.vector.tensor_copy(out=dst, in_=src)
             else:
                 nc.scalar.copy(out=dst, in_=src)
@@ -119,9 +117,9 @@ def tile_minerva_pb_kernel(tc, features, ex_features, g_weight, out_0, out_1):
 
         def front(u):
             if u < len(units):
-                flip(u)
+                transpose(u)
             if 0 <= u - 1 < len(units):
-                regroup(u - 1)
+                copy_out(u - 1)
             if 0 <= u - 2 < len(units):
                 quantise(u - 2)
 
@@ -129,77 +127,72 @@ def tile_minerva_pb_kernel(tc, features, ex_features, g_weight, out_0, out_1):
         result_of = {}
         inverse_of = {}
 
-        def multiply(r, banks):
-            products_of[r] = []
-            for j in range(PAIR):
-                rows = slice((r * PAIR + j) * P, (r * PAIR + j + 1) * P)
-                acc = psum.tile([P, N], F32, name="acc", tag="bank%d" % banks[j])
+        def multiply(pair):
+            products_of[pair] = []
+            for j in range(UNIT):
+                t = pair * UNIT + j
+                acc = psum.tile([P, N], F32, name="acc", tag="bank%d" % (t % PRODUCT_BANKS))
                 nc.tensor.matmul_mx(
                     out=acc[:],
-                    lhsT=x_codes[:, rows].bitcast(FP8X4),
-                    lhsT_scale=x_scales[:, rows],
+                    lhsT=x_codes[:, t * P : (t + 1) * P].bitcast(FP8X4),
+                    lhsT_scale=x_scales[:, t * P : (t + 1) * P],
                     rhs=g_codes[:].bitcast(FP8X4),
                     rhs_scale=g_scales[:],
                     start=True,
                     stop=True,
                 )
-                products_of[r].append(acc)
+                products_of[pair].append(acc)
 
-        def inverse_norms(r):
-            s = r * PAIR // STORE_TILES
-            if r * PAIR % STORE_TILES == 0:
+        def inverse_norms(pair):
+            if pair * UNIT % STORE_TILES == 0:
                 result = result_pool.tile([P, STORE_TILES, N], F32, name="result")
-                result_of[s] = result
-            sumsq = norm_pool.tile([P, PAIR], F32, name="sumsq")
-            for j in range(PAIR):
+                result_of[pair * UNIT // STORE_TILES] = result
+            sumsq = norm_pool.tile([P, UNIT], F32, name="sumsq")
+            for j in range(UNIT):
+                t = pair * UNIT + j
                 nc.scalar.activation(
-                    out=result_of[s][:, (r * PAIR + j) % STORE_TILES, :],
-                    in_=products_of[r][j][:],
+                    out=result_of[t // STORE_TILES][:, t % STORE_TILES, :],
+                    in_=products_of[pair][j][:],
                     func=ACT.Square,
                     accum_out=sumsq[:, j : j + 1],
                 )
-            floored = norm_pool.tile([P, PAIR], F32, name="floored")
+            floored = norm_pool.tile([P, UNIT], F32, name="floored")
             nc.gpsimd.tensor_scalar(
                 out=floored[:], in0=sumsq[:], scalar1=EPS * EPS, scalar2=None, op0=ALU.max
             )
-            inverse = norm_pool.tile([P, PAIR], F32, name="inverse")
+            inverse = norm_pool.tile([P, UNIT], F32, name="inverse")
             nc.gpsimd.tensor_tensor(out=inverse[:], in0=floored[:], in1=minus_half[:], op=ALU.pow)
-            inverse_of[r] = inverse
+            inverse_of[pair] = inverse
 
-        def scale_and_store(r):
-            s = r * PAIR // STORE_TILES
-            for j in range(PAIR):
+        def scale_and_store(pair):
+            for j in range(UNIT):
+                t = pair * UNIT + j
                 nc.vector.tensor_scalar(
-                    out=result_of[s][:, (r * PAIR + j) % STORE_TILES, :],
-                    in0=products_of[r][j][:],
-                    scalar1=inverse_of[r][:, j : j + 1],
+                    out=result_of[t // STORE_TILES][:, t % STORE_TILES, :],
+                    in0=products_of[pair][j][:],
+                    scalar1=inverse_of[pair][:, j : j + 1],
                     scalar2=None,
                     op0=ALU.mult,
                 )
-            done = (r + 1) * PAIR
+            done = (pair + 1) * UNIT
             in_last_store = done > row_tiles - STORE_TILES
             if in_last_store or done % STORE_TILES == 0:
-                count = PAIR if in_last_store else STORE_TILES
-                t0 = (done - count) % GROUP
-                s0 = (done - count) % STORE_TILES
+                count = UNIT if in_last_store else STORE_TILES
+                first = done - count
                 nc.sync.dma_start(
-                    out=out_views[(done - 1) // GROUP][:, t0 : t0 + count, :],
-                    in_=result_of[s][:, s0 : s0 + count, :],
+                    out=out_views[first // GROUP][:, first % GROUP : first % GROUP + count, :],
+                    in_=result_of[first // STORE_TILES][
+                        :, first % STORE_TILES : first % STORE_TILES + count, :
+                    ],
                 )
 
         for u in range(FRONT_LEAD):
             front(u)
-        ring = list(range(PRODUCT_BANKS))
         for i in range(pairs + 2):
-            entered = FRONT_LEAD + FRONT_PER_STEP * i
-            if entered - 1 >= len(units) and len(ring) == PRODUCT_BANKS:
-                ring = list(range(PRODUCT_BANKS, PSUM_BANKS)) + ring
             if 0 <= i - 2:
                 scale_and_store(i - 2)
             if i < pairs:
-                multiply(i, ring[:PAIR])
-                ring = ring[PAIR:] + ring[:PAIR]
+                multiply(i)
             if 0 <= i - 1 < pairs:
                 inverse_norms(i - 1)
-            for u in range(entered, entered + FRONT_PER_STEP):
-                front(u)
+            front(FRONT_LEAD + i)

from contextlib import ExitStack

import concourse.mybir as mybir
from concourse.masks import make_identity

F32 = mybir.dt.float32
BF16 = mybir.dt.bfloat16
U32 = mybir.dt.uint32
U8 = mybir.dt.uint8
FP8X4 = mybir.dt.float8_e4m3fn_x4
ACT = mybir.ActivationFunctionType
ALU = mybir.AluOpType

P = 128
K = 512
N = 512
WORDS = K // 2
UNIT = 2
G_UNITS = N // (UNIT * P)
GROUP = 8
STORE_TILES = 4
PSUM_BANKS = 8
FLIP_BANKS = 2
PRODUCT_BANKS = PSUM_BANKS - FLIP_BANKS
FRONT_LEAD = G_UNITS + 4
VECTOR_COPIES_EVERY = 4
EPS = 1e-12

FLOPS = 2 * (1024 + 8192) * K * N


def tile_minerva_pb_kernel(tc, features, ex_features, g_weight, out_0, out_1):
    nc = tc.nc
    row_tiles = (features.shape[0] + ex_features.shape[0]) // P
    pairs = row_tiles // UNIT
    with ExitStack() as ctx:
        const = ctx.enter_context(tc.tile_pool(name="const", bufs=1))
        rows_pool = ctx.enter_context(tc.tile_pool(name="rows", bufs=1))
        grouped_pool = ctx.enter_context(tc.tile_pool(name="grouped", bufs=3))
        norm_pool = ctx.enter_context(tc.tile_pool(name="norms", bufs=3))
        result_pool = ctx.enter_context(tc.tile_pool(name="result", bufs=8))
        psum = ctx.enter_context(tc.psum_pool(name="psum", bufs=1))
        ctx.enter_context(tc.manual_schedule())

        g_rows = const.tile([P, G_UNITS * UNIT * K], BF16, name="g_rows")
        g_src = g_weight.rearrange("(t p) k -> p t k", p=P)
        g_dst = g_rows[:].rearrange("p (t k) -> p t k", k=K)
        for b in range(G_UNITS):
            tiles = slice(b * UNIT, (b + 1) * UNIT)
            nc.sync.dma_start(out=g_dst[:, tiles, :], in_=g_src[:, tiles, :])
        x_words = []
        out_views = []
        for x, out in ((features, out_0), (ex_features, out_1)):
            for base in range(0, x.shape[0], GROUP * P):
                x_rows = rows_pool.tile([P, GROUP * K], BF16, name="x_rows%d" % len(out_views))
                src = x[base : base + GROUP * P, :].rearrange("(p t) k -> p (t k)", t=GROUP)
                pieces = GROUP // UNIT if len(out_views) == 0 else 1
                width = GROUP * K // pieces
                for c in range(pieces):
                    cols = slice(c * width, (c + 1) * width)
                    nc.sync.dma_start(out=x_rows[:, cols], in_=src[:, cols])
                words = x_rows[:].bitcast(F32)
                for c in range(GROUP // UNIT):
                    x_words.append(words[:, c * UNIT * WORDS : (c + 1) * UNIT * WORDS])
                out_views.append(
                    out[base : base + GROUP * P, :].rearrange("(p t) n -> p t n", t=GROUP)
                )

        identity = const.tile([P, P], F32, name="identity")
        make_identity(nc, identity[:])

        minus_half = const.tile([P, UNIT], F32, name="minus_half")
        nc.vector.memset(minus_half[:], -0.5)

        g_codes = const.tile([P, N], U32, align_bytes=64, name="g_codes")
        g_scales = const.tile([P, N], U8, align_bytes=64, name="g_scales")
        x_codes = const.tile([P, row_tiles * P], U32, align_bytes=64, name="x_codes")
        x_scales = const.tile([P, row_tiles * P], U8, align_bytes=64, name="x_scales")

        g_words = g_rows[:].bitcast(F32)
        units = []
        for b in range(G_UNITS):
            cols = slice(b * UNIT * P, (b + 1) * UNIT * P)
            words = g_words[:, b * UNIT * WORDS : (b + 1) * UNIT * WORDS]
            units.append((words, g_codes[:, cols], g_scales[:, cols]))
        for pair in range(pairs):
            cols = slice(pair * UNIT * P, (pair + 1) * UNIT * P)
            units.append((x_words[pair], x_codes[:, cols], x_scales[:, cols]))

        flipped_of = {}
        grouped_of = {}

        def transpose(u):
            bank = u if u < PRODUCT_BANKS else PRODUCT_BANKS + u % FLIP_BANKS
            flipped = psum.tile([P, UNIT, 2, P], F32, name="flipped", tag="bank%d" % bank)
            words = units[u][0]
            for j in range(UNIT):
                for h in range(2):
                    c = (2 * j + h) * P
                    nc.tensor.transpose(flipped[:, j, h, :], words[:, c : c + P], identity[:])
            flipped_of[u] = flipped

        def copy_out(u):
            grouped = grouped_pool.tile([P, UNIT * K], BF16, align_bytes=64, name="grouped")
            dst = grouped[:].bitcast(F32).rearrange("p (j row h) -> p j row h", j=UNIT, h=2)
            src = flipped_of[u][:].rearrange("p j h row -> p j row h")
            if u % VECTOR_COPIES_EVERY == 0:
                nc.vector.tensor_copy(out=dst, in_=src)
            else:
                nc.scalar.copy(out=dst, in_=src)
            grouped_of[u] = grouped

        def quantise(u):
            nc.vector.quantize_mx(
                out=units[u][1].bitcast(FP8X4), scales=units[u][2], in_=grouped_of[u][:]
            )

        def front(u):
            if u < len(units):
                transpose(u)
            if 0 <= u - 1 < len(units):
                copy_out(u - 1)
            if 0 <= u - 2 < len(units):
                quantise(u - 2)

        products_of = {}
        result_of = {}
        inverse_of = {}

        def multiply(pair):
            products_of[pair] = []
            for j in range(UNIT):
                t = pair * UNIT + j
                acc = psum.tile([P, N], F32, name="acc", tag="bank%d" % (t % PRODUCT_BANKS))
                nc.tensor.matmul_mx(
                    out=acc[:],
                    lhsT=x_codes[:, t * P : (t + 1) * P].bitcast(FP8X4),
                    lhsT_scale=x_scales[:, t * P : (t + 1) * P],
                    rhs=g_codes[:].bitcast(FP8X4),
                    rhs_scale=g_scales[:],
                    start=True,
                    stop=True,
                )
                products_of[pair].append(acc)

        def inverse_norms(pair):
            if pair * UNIT % STORE_TILES == 0:
                result = result_pool.tile([P, STORE_TILES, N], F32, name="result")
                result_of[pair * UNIT // STORE_TILES] = result
            sumsq = norm_pool.tile([P, UNIT], F32, name="sumsq")
            for j in range(UNIT):
                t = pair * UNIT + j
                nc.scalar.activation(
                    out=result_of[t // STORE_TILES][:, t % STORE_TILES, :],
                    in_=products_of[pair][j][:],
                    func=ACT.Square,
                    accum_out=sumsq[:, j : j + 1],
                )
            floored = norm_pool.tile([P, UNIT], F32, name="floored")
            nc.gpsimd.tensor_scalar(
                out=floored[:], in0=sumsq[:], scalar1=EPS * EPS, scalar2=None, op0=ALU.max
            )
            inverse = norm_pool.tile([P, UNIT], F32, name="inverse")
            nc.gpsimd.tensor_tensor(out=inverse[:], in0=floored[:], in1=minus_half[:], op=ALU.pow)
            inverse_of[pair] = inverse

        def scale_and_store(pair):
            for j in range(UNIT):
                t = pair * UNIT + j
                nc.vector.tensor_scalar(
                    out=result_of[t // STORE_TILES][:, t % STORE_TILES, :],
                    in0=products_of[pair][j][:],
                    scalar1=inverse_of[pair][:, j : j + 1],
                    scalar2=None,
                    op0=ALU.mult,
                )
            done = (pair + 1) * UNIT
            in_last_store = done > row_tiles - STORE_TILES
            if in_last_store or done % STORE_TILES == 0:
                count = UNIT if in_last_store else STORE_TILES
                first = done - count
                nc.sync.dma_start(
                    out=out_views[first // GROUP][:, first % GROUP : first % GROUP + count, :],
                    in_=result_of[first // STORE_TILES][
                        :, first % STORE_TILES : first % STORE_TILES + count, :
                    ],
                )

        for u in range(FRONT_LEAD):
            front(u)
        for i in range(pairs + 2):
            if 0 <= i - 2:
                scale_and_store(i - 2)
            if i < pairs:
                multiply(i)
            if 0 <= i - 1 < pairs:
                inverse_norms(i - 1)
            front(FRONT_LEAD + i)
